import numpy as np
import ml_dtypes


def mxq(x, axis, fmt="e4m3"):
    dtype, down = {"e4m3": (ml_dtypes.float8_e4m3fn, 7), "e5m2": (ml_dtypes.float8_e5m2, 14)}[fmt]
    v = np.moveaxis(np.asarray(x, np.float32).astype(ml_dtypes.bfloat16).astype(np.float64), axis, -1)
    blocks = v.reshape(v.shape[:-1] + (-1, 32))
    amax = np.abs(blocks).max(-1, keepdims=True)
    byte = np.maximum(np.where(amax > 0, np.frexp(amax)[1] - 1 + 127, 0) - down, 1)
    scale = np.exp2(byte - 127.0)
    codes = (blocks / scale).astype(np.float32).astype(dtype).astype(np.float64)
    return np.moveaxis((codes * scale).reshape(v.shape), -1, axis)


WIDE = False


def mx_kscale(k):
    if not WIDE:
        return np.ones(k)
    levels = np.array([10, -10, 5, -5, 0])
    a = np.random.permutation(np.resize(levels, k // 512 * 4)).reshape(k // 512, 4)
    idx = np.arange(k)
    return np.exp2(a[idx // 512, idx % 128 // 32])


BF16 = ml_dtypes.bfloat16


def bf(x):
    return np.asarray(x, np.float32).astype(BF16)


def f64(x):
    return np.asarray(x).astype(np.float64)


B, S, D_IN, D_OUT = 2, 256, 2048, 2048


def quant8(w):
    mv = np.max(np.abs(w))
    q = np.ceil(np.log2(mv)) - 6.0
    scale = np.exp2(q)
    return np.round(w / scale) * scale


def setup_inputs():
    s = mx_kscale(D_IN)
    x = np.random.standard_normal((B, S, D_IN))
    weight = np.random.standard_normal((D_OUT, D_IN)) * 3.0 / np.sqrt(D_IN)
    w_upper = quant8(weight)
    w_lower = weight - w_upper
    return {"x": bf(x * s), "weight_upper": bf(w_upper / s[None, :]), "weight_lower": bf(w_lower / s[None, :])}


def reference(x, weight_upper, weight_lower):
    xq = mxq(f64(x), 2, "e4m3")
    y_upper = xq @ mxq(f64(weight_upper), 1, "e4m3").T
    y_lower = xq @ mxq(f64(weight_lower), 1, "e4m3").T
    return y_upper + y_lower

@@ -1,0 +1,134 @@
+from contextlib import ExitStack
+
+import concourse.mybir as mybir
+from concourse.masks import make_identity
+
+BF16 = mybir.dt.bfloat16
+F32 = mybir.dt.float32
+U32 = mybir.dt.uint32
+U8 = mybir.dt.uint8
+FP8X4 = mybir.dt.float8_e4m3fn_x4
+
+P = 128
+TOKENS = 512
+K = 2048
+N_OUT = 2048
+K_PASS = 512
+ROWS = 512
+BLOCKS = ROWS // P
+PASSES = K // K_PASS
+N_TILES = N_OUT // ROWS
+UNITS_PER_RUN = 2
+
+FLOPS = 2 * 2 * TOKENS * K * N_OUT
+
+
+def tile_virtual16bmatmul_kernel(tc, x, weight_upper, weight_lower, out):
+    nc = tc.nc
+    x2 = x.flatten_outer_dims()
+    o2 = out.flatten_outer_dims()
+    with ExitStack() as ctx:
+        const = ctx.enter_context(tc.tile_pool(name="const", bufs=1))
+        raw_pool = ctx.enter_context(tc.tile_pool(name="raw", bufs=1))
+        grp_pool = ctx.enter_context(tc.tile_pool(name="grp", bufs=4))
+        wq_pool = ctx.enter_context(tc.tile_pool(name="wq", bufs=6))
+        res_pool = ctx.enter_context(tc.tile_pool(name="res", bufs=12))
+        psum = ctx.enter_context(tc.psum_pool(name="psum", bufs=1))
+        ctx.enter_context(tc.manual_schedule())
+
+        ident = const.tile([P, P], F32, name="ident")
+        make_identity(nc, ident[:])
+
+        def load(src, row0, k0, klen, name):
+            raw = raw_pool.tile([P, BLOCKS * klen], BF16, name=name)
+            nc.sync.dma_start(
+                out=raw[:].rearrange("p (b k) -> p b k", b=BLOCKS),
+                in_=src[row0 : row0 + ROWS, k0 : k0 + klen].rearrange("(b p) k -> p b k", p=P),
+            )
+            return raw[:].bitcast(F32).rearrange("p (b w) -> p b w", b=BLOCKS)
+
+        units = []
+        for g in range(PASSES):
+            for kind, src in (("x", x2), ("u", weight_upper), ("l", weight_lower)):
+                words = load(src, 0, g * K_PASS, K_PASS, "raw_%s0_%d" % (kind, g))
+                units.append({"kind": kind, "nt": 0, "g": g, "words": words, "w0": 0})
+        for nt in range(1, N_TILES):
+            for kind, src in (("u", weight_upper), ("l", weight_lower)):
+                for h in range(2):
+                    words = load(src, nt * ROWS, h * 2 * K_PASS, 2 * K_PASS, "raw_%s%d_%d" % (kind, nt, h))
+                    for gl in range(2):
+                        units.append({"kind": kind, "nt": nt, "g": 2 * h + gl, "words": words, "w0": gl * (K_PASS // 2)})
+        seen = {}
+        for unit in units:
+            if unit["kind"] != "x":
+                seen[unit["nt"]] = seen.get(unit["nt"], 0) + 1
+                unit["first"] = seen[unit["nt"]] == 1
+                unit["last"] = seen[unit["nt"]] == 2 * PASSES
+
+        x_codes = {}
+        x_scales = {}
+        acc = {}
+
+        def transposes(run):
+            for i, unit in enumerate(run):
+                grouped = grp_pool.tile([P, 4 * ROWS], BF16, name="grouped", align_bytes=64)
+                unit["grouped"] = grouped
+                gwords = grouped[:].bitcast(F32)
+                for h in range(2):
+                    bank = psum.tile([P, 2, 2 * P], F32, name="tp%d" % (2 * i + h), tag="tp%d" % (2 * i + h))
+                    for b in range(2):
+                        for u in range(2):
+                            w0 = unit["w0"] + u * P
+                            nc.tensor.transpose(
+                                bank[:, u, b * P : (b + 1) * P],
+                                unit["words"][:, 2 * h + b, w0 : w0 + P],
+                                ident[:],
+                            )
+                    nc.scalar.copy(
+                        out=gwords[:, h * 4 * P : (h + 1) * 4 * P].rearrange("p (n u) -> p n u", u=2),
+                        in_=bank[:].rearrange("p u n -> p n u"),
+                    )
+
+        def quantise(run):
+            for unit in run:
+                if unit["kind"] == "x":
+                    codes = const.tile([P, ROWS], U32, name="xc%d" % unit["g"], align_bytes=64)
+                    scales = const.tile([P, ROWS], U8, name="xs%d" % unit["g"], align_bytes=64)
+                    x_codes[unit["g"]] = codes
+                    x_scales[unit["g"]] = scales
+                else:
+                    codes = wq_pool.tile([P, ROWS], U32, name="wc", align_bytes=64)
+                    scales = wq_pool.tile([P, ROWS], U8, name="ws", align_bytes=64)
+                    unit["codes"] = codes
+                    unit["scales"] = scales
+                nc.vector.quantize_mx(out=codes[:].bitcast(FP8X4), scales=scales[:], in_=unit["grouped"][:])
+
+        def passes(run):
+            w_units = [unit for unit in run if unit["kind"] != "x"]
+            for tt in range(TOKENS // P):
+                cols = slice(tt * P, (tt + 1) * P)
+                for unit in w_units:
+                    if unit["first"]:
+                        acc[tt] = psum.tile([P, ROWS], F32, name="acc%d" % tt, tag="acc%d" % tt)
+                    nc.tensor.matmul_mx(
+                        out=acc[tt][:],
+                        lhsT=x_codes[unit["g"]][:, cols].bitcast(FP8X4),
+                        lhsT_scale=x_scales[unit["g"]][:, cols],
+                        rhs=unit["codes"][:].bitcast(FP8X4),
+                        rhs_scale=unit["scales"][:],
+                        start=unit["first"],
+                        stop=unit["last"],
+                    )
+                    if unit["last"]:
+                        res = res_pool.tile([P, ROWS], F32, name="res")
+                        nc.vector.tensor_copy(out=res[:], in_=acc[tt][:])
+                        nt = unit["nt"]
+                        nc.sync.dma_start(out=o2[cols, nt * ROWS : (nt + 1) * ROWS], in_=res[:])
+
+        runs = [units[i : i + UNITS_PER_RUN] for i in range(0, len(units), UNITS_PER_RUN)]
+        for j, run in enumerate(runs):
+            transposes(run)
+            quantise(run)
+            if j > 0:
+                passes(runs[j - 1])
+        passes(runs[-1])

@@ -14,11 +14,17 @@ TOKENS = 512
 K = 2048
 N_OUT = 2048
 K_PASS = 512
-ROWS = 512
-BLOCKS = ROWS // P
 PASSES = K // K_PASS
-N_TILES = N_OUT // ROWS
-UNITS_PER_RUN = 2
+TOKEN_TILES = TOKENS // P
+N_COLS = 256
+RANGES = N_OUT // N_COLS
+ROW_WORDS = K // 2
+PASS_WORDS = K_PASS // 2
+
+T_BANKS = 5
+ACC_BANKS = 3
+W_RAW_BUFS = 12
+VECTOR_PASS = 2
 
 FLOPS = 2 * 2 * TOKENS * K * N_OUT
 
@@ -27,108 +33,135 @@ def tile_virtual16bmatmul_kernel(tc, x, weight_upper, weight_lower, out):
     nc = tc.nc
     x2 = x.flatten_outer_dims()
     o2 = out.flatten_outer_dims()
+    weights = {"u": weight_upper, "l": weight_lower}
     with ExitStack() as ctx:
         const = ctx.enter_context(tc.tile_pool(name="const", bufs=1))
-        raw_pool = ctx.enter_context(tc.tile_pool(name="raw", bufs=1))
-        grp_pool = ctx.enter_context(tc.tile_pool(name="grp", bufs=4))
-        wq_pool = ctx.enter_context(tc.tile_pool(name="wq", bufs=6))
-        res_pool = ctx.enter_context(tc.tile_pool(name="res", bufs=12))
+        wraw_pool = ctx.enter_context(tc.tile_pool(name="wraw", bufs=W_RAW_BUFS))
+        grp_pool = ctx.enter_context(tc.tile_pool(name="grp", bufs=3))
+        wq_pool = ctx.enter_context(tc.tile_pool(name="wq", bufs=4))
+        res_pool = ctx.enter_context(tc.tile_pool(name="res", bufs=16))
         psum = ctx.enter_context(tc.psum_pool(name="psum", bufs=1))
         ctx.enter_context(tc.manual_schedule())
 
         ident = const.tile([P, P], F32, name="ident")
         make_identity(nc, ident[:])
 
-        def load(src, row0, k0, klen, name):
-            raw = raw_pool.tile([P, BLOCKS * klen], BF16, name=name)
-            nc.sync.dma_start(
-                out=raw[:].rearrange("p (b k) -> p b k", b=BLOCKS),
-                in_=src[row0 : row0 + ROWS, k0 : k0 + klen].rearrange("(b p) k -> p b k", p=P),
-            )
-            return raw[:].bitcast(F32).rearrange("p (b w) -> p b w", b=BLOCKS)
-
-        units = []
-        for g in range(PASSES):
-            for kind, src in (("x", x2), ("u", weight_upper), ("l", weight_lower)):
-                words = load(src, 0, g * K_PASS, K_PASS, "raw_%s0_%d" % (kind, g))
-                units.append({"kind": kind, "nt": 0, "g": g, "words": words, "w0": 0})
-        for nt in range(1, N_TILES):
-            for kind, src in (("u", weight_upper), ("l", weight_lower)):
-                for h in range(2):
-                    words = load(src, nt * ROWS, h * 2 * K_PASS, 2 * K_PASS, "raw_%s%d_%d" % (kind, nt, h))
-                    for gl in range(2):
-                        units.append({"kind": kind, "nt": nt, "g": 2 * h + gl, "words": words, "w0": gl * (K_PASS // 2)})
-        seen = {}
-        for unit in units:
-            if unit["kind"] != "x":
-                seen[unit["nt"]] = seen.get(unit["nt"], 0) + 1
-                unit["first"] = seen[unit["nt"]] == 1
-                unit["last"] = seen[unit["nt"]] == 2 * PASSES
-
+        x_words = {}
         x_codes = {}
         x_scales = {}
-        acc = {}
+        w_words = {}
+        w_codes = {}
+        w_scales = {}
+        counters = {"tp": 0, "acc": 0, "w": 0}
 
-        def transposes(run):
-            for i, unit in enumerate(run):
-                grouped = grp_pool.tile([P, 4 * ROWS], BF16, name="grouped", align_bytes=64)
-                unit["grouped"] = grouped
-                gwords = grouped[:].bitcast(F32)
-                for h in range(2):
-                    bank = psum.tile([P, 2, 2 * P], F32, name="tp%d" % (2 * i + h), tag="tp%d" % (2 * i + h))
-                    for b in range(2):
-                        for u in range(2):
-                            w0 = unit["w0"] + u * P
-                            nc.tensor.transpose(
-                                bank[:, u, b * P : (b + 1) * P],
-                                unit["words"][:, 2 * h + b, w0 : w0 + P],
-                                ident[:],
-                            )
-                    nc.scalar.copy(
-                        out=gwords[:, h * 4 * P : (h + 1) * 4 * P].rearrange("p (n u) -> p n u", u=2),
-                        in_=bank[:].rearrange("p u n -> p n u"),
-                    )
+        def load_x(tt):
+            raw = const.tile([P, K], BF16, name="xraw%d" % tt)
+            nc.sync.dma_start(out=raw[:], in_=x2[tt * P : (tt + 1) * P, :])
+            x_words[tt] = raw[:].bitcast(F32)
 
-        def quantise(run):
-            for unit in run:
-                if unit["kind"] == "x":
-                    codes = const.tile([P, ROWS], U32, name="xc%d" % unit["g"], align_bytes=64)
-                    scales = const.tile([P, ROWS], U8, name="xs%d" % unit["g"], align_bytes=64)
-                    x_codes[unit["g"]] = codes
-                    x_scales[unit["g"]] = scales
+        def load_w(key):
+            kind, r = key
+            raw = wraw_pool.tile([P, 2 * K], BF16, name="wraw")
+            nc.sync.dma_start(
+                out=raw[:].rearrange("p (b k) -> p b k", b=2),
+                in_=weights[kind][r * N_COLS : (r + 1) * N_COLS, :].rearrange("(b p) k -> p b k", p=P),
+            )
+            w_words[key] = raw[:].bitcast(F32).rearrange("p (b w) -> p b w", b=2)
+
+        def t_bank(shape):
+            i = counters["tp"] % T_BANKS
+            counters["tp"] += 1
+            return psum.tile(shape, F32, name="tp%d" % i, tag="tp%d" % i)
+
+        def transpose_x(tt):
+            grouped = grp_pool.tile([P, 4 * PASSES * P], BF16, name="gx", align_bytes=64)
+            gwords = grouped[:].bitcast(F32)
+            for h in range(2):
+                bank = t_bank([P, 2, 2, P])
+                for g in range(2):
+                    for u in range(2):
+                        w0 = (2 * h + g) * PASS_WORDS + u * P
+                        nc.tensor.transpose(bank[:, g, u, :], x_words[tt][:, w0 : w0 + P], ident[:])
+                nc.scalar.copy(
+                    out=gwords[:, h * 4 * P : (h + 1) * 4 * P].rearrange("p (g n u) -> p g n u", g=2, u=2),
+                    in_=bank[:].rearrange("p g u n -> p g n u"),
+                )
+            codes = const.tile([P, PASSES * P], U32, name="xc%d" % tt, align_bytes=64)
+            scales = const.tile([P, PASSES * P], U8, name="xs%d" % tt, align_bytes=64)
+            nc.vector.quantize_mx(out=codes[:].bitcast(FP8X4), scales=scales[:], in_=grouped[:])
+            x_codes[tt] = codes
+            x_scales[tt] = scales
+
+        def transpose_w(key):
+            grouped = grp_pool.tile([P, 4 * PASSES * N_COLS], BF16, name="gw", align_bytes=64)
+            gwords = grouped[:].bitcast(F32)
+            codes = wq_pool.tile([P, PASSES * N_COLS], U32, name="wc", align_bytes=64)
+            scales = wq_pool.tile([P, PASSES * N_COLS], U8, name="ws", align_bytes=64)
+            for g in range(PASSES):
+                bank = t_bank([P, 2, N_COLS])
+                for b in range(2):
+                    for u in range(2):
+                        w0 = g * PASS_WORDS + u * P
+                        nc.tensor.transpose(bank[:, u, b * P : (b + 1) * P], w_words[key][:, b, w0 : w0 + P], ident[:])
+                dst = gwords[:, g * 2 * N_COLS : (g + 1) * 2 * N_COLS].rearrange("p (n u) -> p n u", u=2)
+                if g == VECTOR_PASS:
+                    nc.vector.tensor_copy(out=dst, in_=bank[:].rearrange("p u n -> p n u"))
                 else:
-                    codes = wq_pool.tile([P, ROWS], U32, name="wc", align_bytes=64)
-                    scales = wq_pool.tile([P, ROWS], U8, name="ws", align_bytes=64)
-                    unit["codes"] = codes
-                    unit["scales"] = scales
-                nc.vector.quantize_mx(out=codes[:].bitcast(FP8X4), scales=scales[:], in_=unit["grouped"][:])
+                    nc.scalar.copy(out=dst, in_=bank[:].rearrange("p u n -> p n u"))
+            for c0 in (0, 2 * N_COLS):
+                nc.vector.quantize_mx(
+                    out=codes[:, c0 : c0 + 2 * N_COLS].bitcast(FP8X4),
+                    scales=scales[:, c0 : c0 + 2 * N_COLS],
+                    in_=grouped[:, 4 * c0 : 4 * (c0 + 2 * N_COLS)],
+                )
+            w_codes[key] = codes
+            w_scales[key] = scales
 
-        def passes(run):
-            w_units = [unit for unit in run if unit["kind"] != "x"]
-            for tt in range(TOKENS // P):
-                cols = slice(tt * P, (tt + 1) * P)
-                for unit in w_units:
-                    if unit["first"]:
-                        acc[tt] = psum.tile([P, ROWS], F32, name="acc%d" % tt, tag="acc%d" % tt)
+        def group(r, tt):
+            i = counters["acc"] % ACC_BANKS
+            counters["acc"] += 1
+            acc = psum.tile([P, N_COLS], F32, name="acc%d" % i, tag="acc%d" % i)
+            for kind in ("u", "l"):
+                for g in range(PASSES):
                     nc.tensor.matmul_mx(
-                        out=acc[tt][:],
-                        lhsT=x_codes[unit["g"]][:, cols].bitcast(FP8X4),
-                        lhsT_scale=x_scales[unit["g"]][:, cols],
-                        rhs=unit["codes"][:].bitcast(FP8X4),
-                        rhs_scale=unit["scales"][:],
-                        start=unit["first"],
-                        stop=unit["last"],
+                        out=acc[:],
+                        lhsT=x_codes[tt][:, g * P : (g + 1) * P].bitcast(FP8X4),
+                        lhsT_scale=x_scales[tt][:, g * P : (g + 1) * P],
+                        rhs=w_codes[(kind, r)][:, g * N_COLS : (g + 1) * N_COLS].bitcast(FP8X4),
+                        rhs_scale=w_scales[(kind, r)][:, g * N_COLS : (g + 1) * N_COLS],
+                        start=(kind == "u" and g == 0),
+                        stop=(kind == "l" and g == PASSES - 1),
                     )
-                    if unit["last"]:
-                        res = res_pool.tile([P, ROWS], F32, name="res")
-                        nc.vector.tensor_copy(out=res[:], in_=acc[tt][:])
-                        nt = unit["nt"]
-                        nc.sync.dma_start(out=o2[cols, nt * ROWS : (nt + 1) * ROWS], in_=res[:])
+            res = res_pool.tile([P, N_COLS], F32, name="res")
+            nc.scalar.copy(out=res[:], in_=acc[:])
+            nc.sync.dma_start(out=o2[tt * P : (tt + 1) * P, r * N_COLS : (r + 1) * N_COLS], in_=res[:])
 
-        runs = [units[i : i + UNITS_PER_RUN] for i in range(0, len(units), UNITS_PER_RUN)]
-        for j, run in enumerate(runs):
-            transposes(run)
-            quantise(run)
-            if j > 0:
-                passes(runs[j - 1])
-        passes(runs[-1])
+        w_keys = [(kind, r) for r in range(RANGES) for kind in ("u", "l")]
+        load_x(0)
+        load_w(w_keys[0])
+        load_w(w_keys[1])
+        for tt in range(1, TOKEN_TILES):
+            load_x(tt)
+        for key in w_keys[2:W_RAW_BUFS]:
+            load_w(key)
+
+        def transposes(r):
+            for kind in ("u", "l"):
+                transpose_w((kind, r))
+                nxt = counters["w"] + W_RAW_BUFS
+                counters["w"] += 1
+                if nxt < len(w_keys):
+                    load_w(w_keys[nxt])
+
+        transpose_x(0)
+        transposes(0)
+        for tt in range(1, TOKEN_TILES):
+            transpose_x(tt)
+            group(0, tt - 1)
+        for r in range(1, RANGES):
+            transposes(r)
+            for tt in range(TOKEN_TILES):
+                if r > 1 or tt == TOKEN_TILES - 1:
+                    group(r - 1, tt)
+        for tt in range(TOKEN_TILES):
+            group(RANGES - 1, tt)

@@ -64,7 +64,7 @@ def tile_virtual16bmatmul_kernel(tc, x, weight_upper, weight_lower, out):
             raw = wraw_pool.tile([P, 2 * K], BF16, name="wraw")
             nc.sync.dma_start(
                 out=raw[:].rearrange("p (b k) -> p b k", b=2),
-                in_=weights[kind][r * N_COLS : (r + 1) * N_COLS, :].rearrange("(b p) k -> p b k", p=P),
+                in_=weights[kind][r * N_COLS : (r + 1) * N_COLS, :].rearrange("(p b) k -> p b k", b=2),
             )
             w_words[key] = raw[:].bitcast(F32).rearrange("p (b w) -> p b w", b=2)
 
@@ -133,7 +133,10 @@ def tile_virtual16bmatmul_kernel(tc, x, weight_upper, weight_lower, out):
                         stop=(kind == "l" and g == PASSES - 1),
                     )
             res = res_pool.tile([P, N_COLS], F32, name="res")
-            nc.scalar.copy(out=res[:], in_=acc[:])
+            nc.scalar.copy(
+                out=res[:].rearrange("m (p b) -> m p b", b=2),
+                in_=acc[:].rearrange("m (b p) -> m p b", b=2),
+            )
             nc.sync.dma_start(out=o2[tt * P : (tt + 1) * P, r * N_COLS : (r + 1) * N_COLS], in_=res[:])
 
         w_keys = [(kind, r) for r in range(RANGES) for kind in ("u", "l")]

@@ -21,10 +21,9 @@ RANGES = N_OUT // N_COLS
 ROW_WORDS = K // 2
 PASS_WORDS = K_PASS // 2
 
-T_BANKS = 5
-ACC_BANKS = 3
+T_BANKS = 6
+ACC_BANKS = 2
 W_RAW_BUFS = 12
-VECTOR_PASS = 2
 
 FLOPS = 2 * 2 * TOKENS * K * N_OUT
 
@@ -50,6 +49,7 @@ def tile_virtual16bmatmul_kernel(tc, x, weight_upper, weight_lower, out):
         x_codes = {}
         x_scales = {}
         w_words = {}
+        w_grouped = {}
         w_codes = {}
         w_scales = {}
         counters = {"tp": 0, "acc": 0, "w": 0}
@@ -73,7 +73,7 @@ def tile_virtual16bmatmul_kernel(tc, x, weight_upper, weight_lower, out):
             counters["tp"] += 1
             return psum.tile(shape, F32, name="tp%d" % i, tag="tp%d" % i)
 
-        def transpose_x(tt):
+        def transpose_x(tt, vector_half=None):
             grouped = grp_pool.tile([P, 4 * PASSES * P], BF16, name="gx", align_bytes=64)
             gwords = grouped[:].bitcast(F32)
             for h in range(2):
@@ -82,21 +82,21 @@ def tile_virtual16bmatmul_kernel(tc, x, weight_upper, weight_lower, out):
                     for u in range(2):
                         w0 = (2 * h + g) * PASS_WORDS + u * P
                         nc.tensor.transpose(bank[:, g, u, :], x_words[tt][:, w0 : w0 + P], ident[:])
-                nc.scalar.copy(
-                    out=gwords[:, h * 4 * P : (h + 1) * 4 * P].rearrange("p (g n u) -> p g n u", g=2, u=2),
-                    in_=bank[:].rearrange("p g u n -> p g n u"),
-                )
+                dst = gwords[:, h * 4 * P : (h + 1) * 4 * P].rearrange("p (g n u) -> p g n u", g=2, u=2)
+                src = bank[:].rearrange("p g u n -> p g n u")
+                if h == vector_half:
+                    nc.vector.tensor_copy(out=dst, in_=src)
+                else:
+                    nc.scalar.copy(out=dst, in_=src)
             codes = const.tile([P, PASSES * P], U32, name="xc%d" % tt, align_bytes=64)
             scales = const.tile([P, PASSES * P], U8, name="xs%d" % tt, align_bytes=64)
             nc.vector.quantize_mx(out=codes[:].bitcast(FP8X4), scales=scales[:], in_=grouped[:])
             x_codes[tt] = codes
             x_scales[tt] = scales
 
-        def transpose_w(key):
+        def transpose_w(key, vector_pass=None):
             grouped = grp_pool.tile([P, 4 * PASSES * N_COLS], BF16, name="gw", align_bytes=64)
             gwords = grouped[:].bitcast(F32)
-            codes = wq_pool.tile([P, PASSES * N_COLS], U32, name="wc", align_bytes=64)
-            scales = wq_pool.tile([P, PASSES * N_COLS], U8, name="ws", align_bytes=64)
             for g in range(PASSES):
                 bank = t_bank([P, 2, N_COLS])
                 for b in range(2):
@@ -104,10 +104,20 @@ def tile_virtual16bmatmul_kernel(tc, x, weight_upper, weight_lower, out):
                         w0 = g * PASS_WORDS + u * P
                         nc.tensor.transpose(bank[:, u, b * P : (b + 1) * P], w_words[key][:, b, w0 : w0 + P], ident[:])
                 dst = gwords[:, g * 2 * N_COLS : (g + 1) * 2 * N_COLS].rearrange("p (n u) -> p n u", u=2)
-                if g == VECTOR_PASS:
+                if g == vector_pass:
                     nc.vector.tensor_copy(out=dst, in_=bank[:].rearrange("p u n -> p n u"))
                 else:
                     nc.scalar.copy(out=dst, in_=bank[:].rearrange("p u n -> p n u"))
+            nxt = counters["w"] + W_RAW_BUFS
+            counters["w"] += 1
+            if nxt < len(w_keys):
+                load_w(w_keys[nxt])
+            w_grouped[key] = grouped
+
+        def quantize_w(key):
+            grouped = w_grouped[key]
+            codes = wq_pool.tile([P, PASSES * N_COLS], U32, name="wc", align_bytes=64)
+            scales = wq_pool.tile([P, PASSES * N_COLS], U8, name="ws", align_bytes=64)
             for c0 in (0, 2 * N_COLS):
                 nc.vector.quantize_mx(
                     out=codes[:, c0 : c0 + 2 * N_COLS].bitcast(FP8X4),
@@ -133,7 +143,7 @@ def tile_virtual16bmatmul_kernel(tc, x, weight_upper, weight_lower, out):
                         stop=(kind == "l" and g == PASSES - 1),
                     )
             res = res_pool.tile([P, N_COLS], F32, name="res")
-            nc.scalar.copy(
+            nc.vector.tensor_copy(
                 out=res[:].rearrange("m (p b) -> m p b", b=2),
                 in_=acc[:].rearrange("m (b p) -> m p b", b=2),
             )
@@ -148,23 +158,26 @@ def tile_virtual16bmatmul_kernel(tc, x, weight_upper, weight_lower, out):
         for key in w_keys[2:W_RAW_BUFS]:
             load_w(key)
 
-        def transposes(r):
-            for kind in ("u", "l"):
-                transpose_w((kind, r))
-                nxt = counters["w"] + W_RAW_BUFS
-                counters["w"] += 1
-                if nxt < len(w_keys):
-                    load_w(w_keys[nxt])
-
-        transpose_x(0)
-        transposes(0)
+        transpose_x(0, 1)
+        for kind in ("u", "l"):
+            transpose_w((kind, 0), 2)
+            quantize_w((kind, 0))
         for tt in range(1, TOKEN_TILES):
             transpose_x(tt)
             group(0, tt - 1)
         for r in range(1, RANGES):
-            transposes(r)
-            for tt in range(TOKEN_TILES):
-                if r > 1 or tt == TOKEN_TILES - 1:
-                    group(r - 1, tt)
+            vector_pass = 2 if r == 1 else None
+            transpose_w(("u", r), vector_pass)
+            transpose_w(("l", r), vector_pass)
+            quantize_w(("u", r))
+            if r == 1:
+                group(0, TOKEN_TILES - 1)
+                quantize_w(("l", r))
+            else:
+                group(r - 1, 0)
+                group(r - 1, 1)
+                quantize_w(("l", r))
+                group(r - 1, 2)
+                group(r - 1, 3)
         for tt in range(TOKEN_TILES):
             group(RANGES - 1, tt)

@@ -25,6 +25,11 @@ T_BANKS = 6
 ACC_BANKS = 2
 W_RAW_BUFS = 12
 
+MIXED = 7
+HALF = N_COLS // 2
+ROW_GROUPS = HALF // 32
+CHUNK_WORDS = 32
+
 FLOPS = 2 * 2 * TOKENS * K * N_OUT
 
 
@@ -36,9 +41,9 @@ def tile_virtual16bmatmul_kernel(tc, x, weight_upper, weight_lower, out):
     with ExitStack() as ctx:
         const = ctx.enter_context(tc.tile_pool(name="const", bufs=1))
         wraw_pool = ctx.enter_context(tc.tile_pool(name="wraw", bufs=W_RAW_BUFS))
-        grp_pool = ctx.enter_context(tc.tile_pool(name="grp", bufs=3))
+        grp_pool = ctx.enter_context(tc.tile_pool(name="grp", bufs=4))
         wq_pool = ctx.enter_context(tc.tile_pool(name="wq", bufs=4))
-        res_pool = ctx.enter_context(tc.tile_pool(name="res", bufs=16))
+        res_pool = ctx.enter_context(tc.tile_pool(name="res", bufs=20))
         psum = ctx.enter_context(tc.psum_pool(name="psum", bufs=1))
         ctx.enter_context(tc.manual_schedule())
 
@@ -50,6 +55,7 @@ def tile_virtual16bmatmul_kernel(tc, x, weight_upper, weight_lower, out):
         x_scales = {}
         w_words = {}
         w_grouped = {}
+        w_turned = {}
         w_codes = {}
         w_scales = {}
         counters = {"tp": 0, "acc": 0, "w": 0}
@@ -58,6 +64,49 @@ def tile_virtual16bmatmul_kernel(tc, x, weight_upper, weight_lower, out):
             raw = const.tile([P, K], BF16, name="xraw%d" % tt)
             nc.sync.dma_start(out=raw[:], in_=x2[tt * P : (tt + 1) * P, :])
             x_words[tt] = raw[:].bitcast(F32)
+
+        def load_mixed(key):
+            kind, r = key
+            rows = weights[kind][r * N_COLS : r * N_COLS + HALF, :]
+            raw = const.tile([P, K], BF16, name="wrow_" + kind)
+            nc.sync.dma_start(out=raw[:], in_=rows)
+            rows = weights[kind][r * N_COLS + HALF : (r + 1) * N_COLS, :]
+            by_quadrant = rows.rearrange("(i v) (c q k) -> q i (v c) k", v=ROW_GROUPS, q=4, k=2 * CHUNK_WORDS)
+            chunks = const.tile([P, K], BF16, name="wchunk_" + kind, align_bytes=64)
+            for q in range(4):
+                nc.sync.dma_start(
+                    out=chunks[32 * q : 32 * (q + 1), :].rearrange("p (c k) -> p c k", k=2 * CHUNK_WORDS),
+                    in_=by_quadrant[q],
+                )
+            w_words[key] = (raw[:].bitcast(F32), chunks[:].bitcast(F32))
+
+        def turn_mixed(key):
+            grouped = grp_pool.tile([P, 4 * PASSES * N_COLS], BF16, name="gw", align_bytes=64)
+            w_grouped[key] = grouped
+            turned = const.tile([P, ROW_WORDS], F32, name="turned_" + key[0], align_bytes=64)
+            nc.vector.transpose(turned[:], w_words[key][1])
+            w_turned[key] = turned
+
+        def interleave_mixed(key):
+            turned = w_turned[key]
+            grouped = w_grouped[key]
+            by_pass = turned[:].rearrange("p (v g u i) -> p g v i u", v=ROW_GROUPS, g=PASSES, u=2)
+            dst = grouped[:].bitcast(F32).rearrange("p (g n u) -> p g n u", g=PASSES, u=2)
+            for g in range(PASSES):
+                nc.scalar.copy(
+                    out=dst[:, g, HALF:, :].rearrange("p (v i) u -> p v i u", v=ROW_GROUPS),
+                    in_=by_pass[:, g],
+                )
+
+        def transpose_mixed(key):
+            dst = w_grouped[key][:].bitcast(F32).rearrange("p (g n u) -> p g n u", g=PASSES, u=2)
+            for h in range(2):
+                bank = t_bank([P, 2, 2, P])
+                for g in range(2):
+                    for u in range(2):
+                        w0 = (2 * h + g) * PASS_WORDS + u * P
+                        nc.tensor.transpose(bank[:, g, u, :], w_words[key][0][:, w0 : w0 + P], ident[:])
+                nc.scalar.copy(out=dst[:, 2 * h : 2 * h + 2, 0:HALF, :], in_=bank[:].rearrange("p g u n -> p g n u"))
 
         def load_w(key):
             kind, r = key
@@ -143,13 +192,21 @@ def tile_virtual16bmatmul_kernel(tc, x, weight_upper, weight_lower, out):
                         stop=(kind == "l" and g == PASSES - 1),
                     )
             res = res_pool.tile([P, N_COLS], F32, name="res")
-            nc.vector.tensor_copy(
-                out=res[:].rearrange("m (p b) -> m p b", b=2),
-                in_=acc[:].rearrange("m (b p) -> m p b", b=2),
-            )
+            if r == MIXED:
+                nc.vector.tensor_copy(out=res[:, 0:HALF], in_=acc[:, 0:HALF])
+                nc.vector.tensor_copy(
+                    out=res[:, HALF:].rearrange("m (i v) -> m i v", v=ROW_GROUPS),
+                    in_=acc[:, HALF:].rearrange("m (v i) -> m i v", v=ROW_GROUPS),
+                )
+            else:
+                nc.vector.tensor_copy(
+                    out=res[:].rearrange("m (p b) -> m p b", b=2),
+                    in_=acc[:].rearrange("m (b p) -> m p b", b=2),
+                )
             nc.sync.dma_start(out=o2[tt * P : (tt + 1) * P, r * N_COLS : (r + 1) * N_COLS], in_=res[:])
 
-        w_keys = [(kind, r) for r in range(RANGES) for kind in ("u", "l")]
+        w_keys = [(kind, r) for r in range(RANGES) if r != MIXED for kind in ("u", "l")]
+        mixed_keys = [("u", MIXED), ("l", MIXED)]
         load_x(0)
         load_w(w_keys[0])
         load_w(w_keys[1])
@@ -162,13 +219,28 @@ def tile_virtual16bmatmul_kernel(tc, x, weight_upper, weight_lower, out):
         for kind in ("u", "l"):
             transpose_w((kind, 0), 2)
             quantize_w((kind, 0))
+        for key in mixed_keys:
+            load_mixed(key)
         for tt in range(1, TOKEN_TILES):
             transpose_x(tt)
             group(0, tt - 1)
         for r in range(1, RANGES):
-            vector_pass = 2 if r == 1 else None
-            transpose_w(("u", r), vector_pass)
-            transpose_w(("l", r), vector_pass)
+            if r == MIXED:
+                for key in mixed_keys:
+                    transpose_mixed(key)
+                interleave_mixed(mixed_keys[1])
+            else:
+                vector_pass = 2 if r == 1 else None
+                transpose_w(("u", r), vector_pass)
+                transpose_w(("l", r), vector_pass)
+            if r == MIXED:
+                group(r - 1, 0)
+                quantize_w(("u", r))
+                group(r - 1, 1)
+                group(r - 1, 2)
+                quantize_w(("l", r))
+                group(r - 1, 3)
+                continue
             quantize_w(("u", r))
             if r == 1:
                 group(0, TOKEN_TILES - 1)
@@ -176,8 +248,13 @@ def tile_virtual16bmatmul_kernel(tc, x, weight_upper, weight_lower, out):
             else:
                 group(r - 1, 0)
                 group(r - 1, 1)
+                if r == MIXED - 1:
+                    turn_mixed(("u", MIXED))
+                    interleave_mixed(("u", MIXED))
                 quantize_w(("l", r))
                 group(r - 1, 2)
                 group(r - 1, 3)
+                if r == MIXED - 1:
+                    turn_mixed(("l", MIXED))
         for tt in range(TOKEN_TILES):
             group(RANGES - 1, tt)

from contextlib import ExitStack

import concourse.mybir as mybir
from concourse.masks import make_identity

BF16 = mybir.dt.bfloat16
F32 = mybir.dt.float32
U32 = mybir.dt.uint32
U8 = mybir.dt.uint8
FP8X4 = mybir.dt.float8_e4m3fn_x4

P = 128
TOKENS = 512
K = 2048
N_OUT = 2048
K_PASS = 512
PASSES = K // K_PASS
TOKEN_TILES = TOKENS // P
N_COLS = 256
RANGES = N_OUT // N_COLS
ROW_WORDS = K // 2
PASS_WORDS = K_PASS // 2

T_BANKS = 6
ACC_BANKS = 2
W_RAW_BUFS = 12

MIXED = 7
HALF = N_COLS // 2
ROW_GROUPS = HALF // 32
CHUNK_WORDS = 32

FLOPS = 2 * 2 * TOKENS * K * N_OUT


def tile_virtual16bmatmul_kernel(tc, x, weight_upper, weight_lower, out):
    nc = tc.nc
    x2 = x.flatten_outer_dims()
    o2 = out.flatten_outer_dims()
    weights = {"u": weight_upper, "l": weight_lower}
    with ExitStack() as ctx:
        const = ctx.enter_context(tc.tile_pool(name="const", bufs=1))
        wraw_pool = ctx.enter_context(tc.tile_pool(name="wraw", bufs=W_RAW_BUFS))
        grp_pool = ctx.enter_context(tc.tile_pool(name="grp", bufs=4))
        wq_pool = ctx.enter_context(tc.tile_pool(name="wq", bufs=4))
        res_pool = ctx.enter_context(tc.tile_pool(name="res", bufs=20))
        psum = ctx.enter_context(tc.psum_pool(name="psum", bufs=1))
        ctx.enter_context(tc.manual_schedule())

        ident = const.tile([P, P], F32, name="ident")
        make_identity(nc, ident[:])

        x_words = {}
        x_codes = {}
        x_scales = {}
        w_words = {}
        w_grouped = {}
        w_turned = {}
        w_codes = {}
        w_scales = {}
        counters = {"tp": 0, "acc": 0, "w": 0}

        def load_x(tt):
            raw = const.tile([P, K], BF16, name="xraw%d" % tt)
            nc.sync.dma_start(out=raw[:], in_=x2[tt * P : (tt + 1) * P, :])
            x_words[tt] = raw[:].bitcast(F32)

        def load_mixed(key):
            kind, r = key
            rows = weights[kind][r * N_COLS : r * N_COLS + HALF, :]
            raw = const.tile([P, K], BF16, name="wrow_" + kind)
            nc.sync.dma_start(out=raw[:], in_=rows)
            rows = weights[kind][r * N_COLS + HALF : (r + 1) * N_COLS, :]
            by_quadrant = rows.rearrange("(i v) (c q k) -> q i (v c) k", v=ROW_GROUPS, q=4, k=2 * CHUNK_WORDS)
            chunks = const.tile([P, K], BF16, name="wchunk_" + kind, align_bytes=64)
            for q in range(4):
                nc.sync.dma_start(
                    out=chunks[32 * q : 32 * (q + 1), :].rearrange("p (c k) -> p c k", k=2 * CHUNK_WORDS),
                    in_=by_quadrant[q],
                )
            w_words[key] = (raw[:].bitcast(F32), chunks[:].bitcast(F32))

        def turn_mixed(key):
            grouped = grp_pool.tile([P, 4 * PASSES * N_COLS], BF16, name="gw", align_bytes=64)
            w_grouped[key] = grouped
            turned = const.tile([P, ROW_WORDS], F32, name="turned_" + key[0], align_bytes=64)
            nc.vector.transpose(turned[:], w_words[key][1])
            w_turned[key] = turned

        def interleave_mixed(key):
            turned = w_turned[key]
            grouped = w_grouped[key]
            by_pass = turned[:].rearrange("p (v g u i) -> p g v i u", v=ROW_GROUPS, g=PASSES, u=2)
            dst = grouped[:].bitcast(F32).rearrange("p (g n u) -> p g n u", g=PASSES, u=2)
            for g in range(PASSES):
                nc.scalar.copy(
                    out=dst[:, g, HALF:, :].rearrange("p (v i) u -> p v i u", v=ROW_GROUPS),
                    in_=by_pass[:, g],
                )

        def transpose_mixed(key):
            dst = w_grouped[key][:].bitcast(F32).rearrange("p (g n u) -> p g n u", g=PASSES, u=2)
            for h in range(2):
                bank = t_bank([P, 2, 2, P])
                for g in range(2):
                    for u in range(2):
                        w0 = (2 * h + g) * PASS_WORDS + u * P
                        nc.tensor.transpose(bank[:, g, u, :], w_words[key][0][:, w0 : w0 + P], ident[:])
                nc.scalar.copy(out=dst[:, 2 * h : 2 * h + 2, 0:HALF, :], in_=bank[:].rearrange("p g u n -> p g n u"))

        def load_w(key):
            kind, r = key
            raw = wraw_pool.tile([P, 2 * K], BF16, name="wraw")
            nc.sync.dma_start(
                out=raw[:].rearrange("p (b k) -> p b k", b=2),
                in_=weights[kind][r * N_COLS : (r + 1) * N_COLS, :].rearrange("(p b) k -> p b k", b=2),
            )
            w_words[key] = raw[:].bitcast(F32).rearrange("p (b w) -> p b w", b=2)

        def t_bank(shape):
            i = counters["tp"] % T_BANKS
            counters["tp"] += 1
            return psum.tile(shape, F32, name="tp%d" % i, tag="tp%d" % i)

        def transpose_x(tt, vector_half=None):
            grouped = grp_pool.tile([P, 4 * PASSES * P], BF16, name="gx", align_bytes=64)
            gwords = grouped[:].bitcast(F32)
            for h in range(2):
                bank = t_bank([P, 2, 2, P])
                for g in range(2):
                    for u in range(2):
                        w0 = (2 * h + g) * PASS_WORDS + u * P
                        nc.tensor.transpose(bank[:, g, u, :], x_words[tt][:, w0 : w0 + P], ident[:])
                dst = gwords[:, h * 4 * P : (h + 1) * 4 * P].rearrange("p (g n u) -> p g n u", g=2, u=2)
                src = bank[:].rearrange("p g u n -> p g n u")
                if h == vector_half:
                    nc.vector.tensor_copy(out=dst, in_=src)
                else:
                    nc.scalar.copy(out=dst, in_=src)
            codes = const.tile([P, PASSES * P], U32, name="xc%d" % tt, align_bytes=64)
            scales = const.tile([P, PASSES * P], U8, name="xs%d" % tt, align_bytes=64)
            nc.vector.quantize_mx(out=codes[:].bitcast(FP8X4), scales=scales[:], in_=grouped[:])
            x_codes[tt] = codes
            x_scales[tt] = scales

        def transpose_w(key, vector_pass=None):
            grouped = grp_pool.tile([P, 4 * PASSES * N_COLS], BF16, name="gw", align_bytes=64)
            gwords = grouped[:].bitcast(F32)
            for g in range(PASSES):
                bank = t_bank([P, 2, N_COLS])
                for b in range(2):
                    for u in range(2):
                        w0 = g * PASS_WORDS + u * P
                        nc.tensor.transpose(bank[:, u, b * P : (b + 1) * P], w_words[key][:, b, w0 : w0 + P], ident[:])
                dst = gwords[:, g * 2 * N_COLS : (g + 1) * 2 * N_COLS].rearrange("p (n u) -> p n u", u=2)
                if g == vector_pass:
                    nc.vector.tensor_copy(out=dst, in_=bank[:].rearrange("p u n -> p n u"))
                else:
                    nc.scalar.copy(out=dst, in_=bank[:].rearrange("p u n -> p n u"))
            nxt = counters["w"] + W_RAW_BUFS
            counters["w"] += 1
            if nxt < len(w_keys):
                load_w(w_keys[nxt])
            w_grouped[key] = grouped

        def quantize_w(key):
            grouped = w_grouped[key]
            codes = wq_pool.tile([P, PASSES * N_COLS], U32, name="wc", align_bytes=64)
            scales = wq_pool.tile([P, PASSES * N_COLS], U8, name="ws", align_bytes=64)
            for c0 in (0, 2 * N_COLS):
                nc.vector.quantize_mx(
                    out=codes[:, c0 : c0 + 2 * N_COLS].bitcast(FP8X4),
                    scales=scales[:, c0 : c0 + 2 * N_COLS],
                    in_=grouped[:, 4 * c0 : 4 * (c0 + 2 * N_COLS)],
                )
            w_codes[key] = codes
            w_scales[key] = scales

        def group(r, tt):
            i = counters["acc"] % ACC_BANKS
            counters["acc"] += 1
            acc = psum.tile([P, N_COLS], F32, name="acc%d" % i, tag="acc%d" % i)
            for kind in ("u", "l"):
                for g in range(PASSES):
                    nc.tensor.matmul_mx(
                        out=acc[:],
                        lhsT=x_codes[tt][:, g * P : (g + 1) * P].bitcast(FP8X4),
                        lhsT_scale=x_scales[tt][:, g * P : (g + 1) * P],
                        rhs=w_codes[(kind, r)][:, g * N_COLS : (g + 1) * N_COLS].bitcast(FP8X4),
                        rhs_scale=w_scales[(kind, r)][:, g * N_COLS : (g + 1) * N_COLS],
                        start=(kind == "u" and g == 0),
                        stop=(kind == "l" and g == PASSES - 1),
                    )
            res = res_pool.tile([P, N_COLS], F32, name="res")
            if r == MIXED:
                nc.vector.tensor_copy(out=res[:, 0:HALF], in_=acc[:, 0:HALF])
                nc.vector.tensor_copy(
                    out=res[:, HALF:].rearrange("m (i v) -> m i v", v=ROW_GROUPS),
                    in_=acc[:, HALF:].rearrange("m (v i) -> m i v", v=ROW_GROUPS),
                )
            else:
                nc.vector.tensor_copy(
                    out=res[:].rearrange("m (p b) -> m p b", b=2),
                    in_=acc[:].rearrange("m (b p) -> m p b", b=2),
                )
            nc.sync.dma_start(out=o2[tt * P : (tt + 1) * P, r * N_COLS : (r + 1) * N_COLS], in_=res[:])

        w_keys = [(kind, r) for r in range(RANGES) if r != MIXED for kind in ("u", "l")]
        mixed_keys = [("u", MIXED), ("l", MIXED)]
        load_x(0)
        load_w(w_keys[0])
        load_w(w_keys[1])
        for tt in range(1, TOKEN_TILES):
            load_x(tt)
        for key in w_keys[2:W_RAW_BUFS]:
            load_w(key)

        transpose_x(0, 1)
        for kind in ("u", "l"):
            transpose_w((kind, 0), 2)
            quantize_w((kind, 0))
        for key in mixed_keys:
            load_mixed(key)
        for tt in range(1, TOKEN_TILES):
            transpose_x(tt)
            group(0, tt - 1)
        for r in range(1, RANGES):
            if r == MIXED:
                for key in mixed_keys:
                    transpose_mixed(key)
                interleave_mixed(mixed_keys[1])
            else:
                vector_pass = 2 if r == 1 else None
                transpose_w(("u", r), vector_pass)
                transpose_w(("l", r), vector_pass)
            if r == MIXED:
                group(r - 1, 0)
                quantize_w(("u", r))
                group(r - 1, 1)
                group(r - 1, 2)
                quantize_w(("l", r))
                group(r - 1, 3)
                continue
            quantize_w(("u", r))
            if r == 1:
                group(0, TOKEN_TILES - 1)
                quantize_w(("l", r))
            else:
                group(r - 1, 0)
                group(r - 1, 1)
                if r == MIXED - 1:
                    turn_mixed(("u", MIXED))
                    interleave_mixed(("u", MIXED))
                quantize_w(("l", r))
                group(r - 1, 2)
                group(r - 1, 3)
                if r == MIXED - 1:
                    turn_mixed(("l", MIXED))
        for tt in range(TOKEN_TILES):
            group(RANGES - 1, tt)
